import numpy as np
import ml_dtypes


def mxq(x, axis, fmt="e4m3"):
    dtype, down = {"e4m3": (ml_dtypes.float8_e4m3fn, 7), "e5m2": (ml_dtypes.float8_e5m2, 14)}[fmt]
    v = np.moveaxis(np.asarray(x, np.float32).astype(ml_dtypes.bfloat16).astype(np.float64), axis, -1)
    blocks = v.reshape(v.shape[:-1] + (-1, 32))
    amax = np.abs(blocks).max(-1, keepdims=True)
    byte = np.maximum(np.where(amax > 0, np.frexp(amax)[1] - 1 + 127, 0) - down, 1)
    scale = np.exp2(byte - 127.0)
    codes = (blocks / scale).astype(np.float32).astype(dtype).astype(np.float64)
    return np.moveaxis((codes * scale).reshape(v.shape), -1, axis)


WIDE = False


def mx_kscale(k):
    if not WIDE:
        return np.ones(k)
    levels = np.array([10, -10, 5, -5, 0])
    a = np.random.permutation(np.resize(levels, k // 512 * 4)).reshape(k // 512, 4)
    idx = np.arange(k)
    return np.exp2(a[idx // 512, idx % 128 // 32])


BF16 = ml_dtypes.bfloat16


def bf(x):
    return np.asarray(x, np.float32).astype(BF16)


def f64(x):
    return np.asarray(x).astype(np.float64)


B, C, N, T, E, O, KCH, ORD = 2, 64, 1024, 12, 10, 64, 3, 2
SIG = 3.0


def setup_inputs():
    s = mx_kscale(N)
    w = np.exp(SIG * np.random.standard_normal((N, N)))
    adj = w / w.sum(-1, keepdims=True)
    return {"x": bf(np.random.standard_normal((B, C, N, T)) / s[None, None, :, None]),
            "adj": bf(adj * s[:, None] / s[None, :])}


def reference(x, adj):
    R = B * C * T
    xr = f64(x).transpose(0, 1, 3, 2).reshape(R, N)
    aq = mxq(f64(adj), 0, "e4m3")
    x1 = mxq(xr, 1, "e4m3") @ aq
    x2 = mxq(x1, 1, "e4m3") @ aq
    return (x1.reshape(B, C, T, N).transpose(0, 1, 3, 2), x2.reshape(B, C, T, N).transpose(0, 1, 3, 2))

@@ -1,0 +1,151 @@
+import concourse.mybir as mybir
+from concourse.masks import make_identity
+
+F32 = mybir.dt.float32
+BF16 = mybir.dt.bfloat16
+U32 = mybir.dt.uint32
+U8 = mybir.dt.uint8
+FP8X4 = mybir.dt.float8_e4m3fn_x4
+
+P = 128
+PACK = 4
+NODES = 1024
+STEPS = 12
+ROWS = 128
+PASSES = NODES // (P * PACK)
+NODE_TILES = NODES // P
+PAIRS = STEPS // 2
+QUARTERS = 4
+STEP_GROUPS = STEPS // QUARTERS
+
+FLOPS = 2 * 2 * ROWS * STEPS * NODES * NODES
+
+
+def copy_out(nc, on_scalar, out, in_):
+    if on_scalar:
+        nc.scalar.copy(out=out, in_=in_)
+    else:
+        nc.vector.tensor_copy(out=out, in_=in_)
+
+
+def hop_to_output(nc, psum, stage, feat_codes, feat_scales, adj_codes, adj_scales, out_rows):
+    for wt in range(NODE_TILES):
+        w_cols = slice(wt * P, (wt + 1) * P)
+        rows = stage.tile([ROWS, P, STEPS], F32, name="rows")
+        for g in range(STEP_GROUPS):
+            bank = psum.tile([ROWS, QUARTERS, P], F32, name="bank", tag="bank")
+            for i in range(QUARTERS):
+                step = g * QUARTERS + i
+                for c in range(PASSES):
+                    nc.tensor.matmul_mx(
+                        out=bank[:, i, :],
+                        lhsT=feat_codes[:, c, step, :].bitcast(FP8X4),
+                        lhsT_scale=feat_scales[:, c, step, :],
+                        rhs=adj_codes[:, c, w_cols].bitcast(FP8X4),
+                        rhs_scale=adj_scales[:, c, w_cols],
+                        start=(c == 0),
+                        stop=(c == PASSES - 1),
+                    )
+            copy_out(
+                nc,
+                wt % 2 == 0,
+                rows[:, :, g * QUARTERS : (g + 1) * QUARTERS],
+                bank[:].rearrange("r i w -> r w i"),
+            )
+        nc.sync.dma_start(
+            out=out_rows[:, wt * P * STEPS : (wt + 1) * P * STEPS],
+            in_=rows[:].rearrange("r w l -> r (w l)"),
+        )
+
+
+def tile_avwgcn_pb_kernel(tc, x, adj, out_0, out_1):
+    nc = tc.nc
+    x_rows = x.rearrange("b c v l -> (b c) (v l)")
+    adj_rows = adj.rearrange("(c t p) w -> p c t w", c=PASSES, t=PACK, p=P)
+    x1_rows = out_0.rearrange("b c w l -> (b c) (w l)")
+    x2_rows = out_1.rearrange("b c w l -> (b c) (w l)")
+    half = NODES * STEPS // PASSES
+
+    with tc.tile_pool(name="keep", bufs=1) as keep, tc.tile_pool(
+        name="stage", bufs=6
+    ) as stage, tc.psum_pool(name="psum", bufs=8) as psum:
+        identity = keep.tile([P, P], F32, name="identity")
+        make_identity(nc, identity[:])
+
+        adj_raw = keep.tile([P, PASSES, PACK, NODES], BF16, name="adj_raw")
+        x_raw = keep.tile([ROWS, PASSES, half], BF16, name="x_raw")
+        for c in range(PASSES):
+            nc.sync.dma_start(out=adj_raw[:, c], in_=adj_rows[:, c])
+        for c in range(PASSES):
+            nc.sync.dma_start(out=x_raw[:, c, :], in_=x_rows[:, c * half : (c + 1) * half])
+
+        adj_grouped = keep.tile([P, PASSES, NODES, PACK], BF16, name="adj_grouped", align_bytes=64)
+        adj_codes = keep.tile([P, PASSES, NODES], U32, name="adj_codes", align_bytes=64)
+        adj_scales = keep.tile([P, PASSES, NODES], U8, name="adj_scales", align_bytes=64)
+        for c in range(PASSES):
+            nc.vector.tensor_copy(
+                out=adj_grouped[:, c].rearrange("p (n i) t -> p n t i", i=4),
+                in_=adj_raw[:, c].rearrange("p t (n i) -> p n t i", i=4),
+            )
+        for c in range(PASSES):
+            nc.vector.quantize_mx(
+                out=adj_codes[:, c, :].bitcast(FP8X4),
+                scales=adj_scales[:, c, :],
+                in_=adj_grouped[:, c].rearrange("p w t -> p (w t)"),
+            )
+
+        x_words = x_raw[:].bitcast(F32).rearrange("r c (t p q) -> r c t p q", t=PACK, p=P, q=PAIRS)
+        x_grouped = keep.tile([P, PASSES, STEPS, ROWS, PACK], BF16, name="x_grouped", align_bytes=64)
+        x_codes = keep.tile([P, PASSES, STEPS, ROWS], U32, name="x_codes", align_bytes=64)
+        x_scales = keep.tile([P, PASSES, STEPS, ROWS], U8, name="x_scales", align_bytes=64)
+        for c in range(PASSES):
+            for q in range(PAIRS):
+                bank = psum.tile([P, PACK, ROWS], F32, name="bank", tag="bank")
+                for t in range(PACK):
+                    nc.tensor.transpose(bank[:, t, :], x_words[:, c, t, :, q], identity[:])
+                copy_out(
+                    nc,
+                    c == 0,
+                    x_grouped[:, c, 2 * q : 2 * q + 2],
+                    bank[:].bitcast(BF16).rearrange("p t (r e) -> p e r t", e=2),
+                )
+                nc.vector.quantize_mx(
+                    out=x_codes[:, c, 2 * q : 2 * q + 2].rearrange("p l r -> p (l r)").bitcast(FP8X4),
+                    scales=x_scales[:, c, 2 * q : 2 * q + 2].rearrange("p l r -> p (l r)"),
+                    in_=x_grouped[:, c, 2 * q : 2 * q + 2].rearrange("p l r t -> p (l r t)"),
+                )
+
+        x1_grouped = keep.tile([P, PASSES, STEPS, ROWS, PACK], BF16, name="x1_grouped", align_bytes=64)
+        x1_codes = keep.tile([P, PASSES, STEPS, ROWS], U32, name="x1_codes", align_bytes=64)
+        x1_scales = keep.tile([P, PASSES, STEPS, ROWS], U8, name="x1_scales", align_bytes=64)
+        for g in range(STEP_GROUPS):
+            steps = slice(g * QUARTERS, (g + 1) * QUARTERS)
+            for c2 in range(PASSES):
+                for step in range(g * QUARTERS, (g + 1) * QUARTERS):
+                    bank = psum.tile([P, PACK, ROWS], F32, name="bank", tag="bank")
+                    for t in range(PACK):
+                        w_cols = slice((c2 * PACK + t) * P, (c2 * PACK + t + 1) * P)
+                        for c in range(PASSES):
+                            nc.tensor.matmul_mx(
+                                out=bank[:, t, :],
+                                lhsT=adj_codes[:, c, w_cols].bitcast(FP8X4),
+                                lhsT_scale=adj_scales[:, c, w_cols],
+                                rhs=x_codes[:, c, step, :].bitcast(FP8X4),
+                                rhs_scale=x_scales[:, c, step, :],
+                                start=(c == 0),
+                                stop=(c == PASSES - 1),
+                            )
+                    copy_out(
+                        nc,
+                        step % 3 != 2,
+                        x1_grouped[:, c2, step],
+                        bank[:].rearrange("p t r -> p r t"),
+                    )
+                nc.vector.quantize_mx(
+                    out=x1_codes[:, c2, steps].rearrange("p l r -> p (l r)").bitcast(FP8X4),
+                    scales=x1_scales[:, c2, steps].rearrange("p l r -> p (l r)"),
+                    in_=x1_grouped[:, c2, steps].rearrange("p l r t -> p (l r t)"),
+                )
+
+        hop_to_output(nc, psum, stage, x_codes, x_scales, adj_codes, adj_scales, x1_rows)
+        hop_to_output(nc, psum, stage, x1_codes, x1_scales, adj_codes, adj_scales, x2_rows)

@@ -67,8 +67,10 @@ def tile_avwgcn_pb_kernel(tc, x, adj, out_0, out_1):
     half = NODES * STEPS // PASSES
 
     with tc.tile_pool(name="keep", bufs=1) as keep, tc.tile_pool(
-        name="stage", bufs=6
-    ) as stage, tc.psum_pool(name="psum", bufs=8) as psum:
+        name="mid", bufs=6
+    ) as mid, tc.tile_pool(name="stage", bufs=4) as stage, tc.psum_pool(
+        name="psum", bufs=8
+    ) as psum:
         identity = keep.tile([P, P], F32, name="identity")
         make_identity(nc, identity[:])
 
@@ -105,7 +107,7 @@ def tile_avwgcn_pb_kernel(tc, x, adj, out_0, out_1):
                     nc.tensor.transpose(bank[:, t, :], x_words[:, c, t, :, q], identity[:])
                 copy_out(
                     nc,
-                    c == 0,
+                    q % 3 != 2,
                     x_grouped[:, c, 2 * q : 2 * q + 2],
                     bank[:].bitcast(BF16).rearrange("p t (r e) -> p e r t", e=2),
                 )
@@ -118,34 +120,55 @@ def tile_avwgcn_pb_kernel(tc, x, adj, out_0, out_1):
         x1_grouped = keep.tile([P, PASSES, STEPS, ROWS, PACK], BF16, name="x1_grouped", align_bytes=64)
         x1_codes = keep.tile([P, PASSES, STEPS, ROWS], U32, name="x1_codes", align_bytes=64)
         x1_scales = keep.tile([P, PASSES, STEPS, ROWS], U8, name="x1_scales", align_bytes=64)
-        for g in range(STEP_GROUPS):
-            steps = slice(g * QUARTERS, (g + 1) * QUARTERS)
-            for c2 in range(PASSES):
-                for step in range(g * QUARTERS, (g + 1) * QUARTERS):
-                    bank = psum.tile([P, PACK, ROWS], F32, name="bank", tag="bank")
-                    for t in range(PACK):
-                        w_cols = slice((c2 * PACK + t) * P, (c2 * PACK + t + 1) * P)
-                        for c in range(PASSES):
-                            nc.tensor.matmul_mx(
-                                out=bank[:, t, :],
-                                lhsT=adj_codes[:, c, w_cols].bitcast(FP8X4),
-                                lhsT_scale=adj_scales[:, c, w_cols],
-                                rhs=x_codes[:, c, step, :].bitcast(FP8X4),
-                                rhs_scale=x_scales[:, c, step, :],
-                                start=(c == 0),
-                                stop=(c == PASSES - 1),
-                            )
-                    copy_out(
-                        nc,
-                        step % 3 != 2,
-                        x1_grouped[:, c2, step],
-                        bank[:].rearrange("p t r -> p r t"),
-                    )
+        for c2 in range(PASSES):
+            sums = []
+            for g in range(STEP_GROUPS):
+                steps = slice(g * QUARTERS, (g + 1) * QUARTERS)
+                x1_t = mid.tile([P, PACK, QUARTERS, ROWS], F32, name="x1_t")
+                sums.append(x1_t)
+                for t in range(PACK):
+                    w_cols = slice((c2 * PACK + t) * P, (c2 * PACK + t + 1) * P)
+                    bank = psum.tile([P, QUARTERS, ROWS], F32, name="bank", tag="bank")
+                    for c in range(PASSES):
+                        nc.tensor.matmul_mx(
+                            out=bank[:].rearrange("p i r -> p (i r)"),
+                            lhsT=adj_codes[:, c, w_cols].bitcast(FP8X4),
+                            lhsT_scale=adj_scales[:, c, w_cols],
+                            rhs=x_codes[:, c, steps].rearrange("p l r -> p (l r)").bitcast(FP8X4),
+                            rhs_scale=x_scales[:, c, steps].rearrange("p l r -> p (l r)"),
+                            start=(c == 0),
+                            stop=(c == PASSES - 1),
+                        )
+                    copy_out(nc, (g * PACK + t) % 3 != 2, x1_t[:, t], bank[:])
+                nc.gpsimd.tensor_scalar(
+                    out=x1_grouped[:, c2, steps],
+                    in0=x1_t[:].rearrange("p t i r -> p i r t"),
+                    scalar1=1.0,
+                    scalar2=0.0,
+                    op0=mybir.AluOpType.mult,
+                    op1=mybir.AluOpType.add,
+                )
                 nc.vector.quantize_mx(
                     out=x1_codes[:, c2, steps].rearrange("p l r -> p (l r)").bitcast(FP8X4),
                     scales=x1_scales[:, c2, steps].rearrange("p l r -> p (l r)"),
                     in_=x1_grouped[:, c2, steps].rearrange("p l r t -> p (l r t)"),
                 )
+            for t in range(PACK):
+                wt = c2 * PACK + t
+                rows = stage.tile([ROWS, P, STEPS], F32, name="rows")
+                for g in range(STEP_GROUPS):
+                    bank = psum.tile([ROWS, QUARTERS, P], F32, name="bank", tag="bank")
+                    for i in range(QUARTERS):
+                        nc.tensor.transpose(bank[:, i, :], sums[g][:, t, i, :], identity[:])
+                    copy_out(
+                        nc,
+                        wt % 2 == 0,
+                        rows[:, :, g * QUARTERS : (g + 1) * QUARTERS],
+                        bank[:].rearrange("r i w -> r w i"),
+                    )
+                nc.sync.dma_start(
+                    out=x1_rows[:, wt * P * STEPS : (wt + 1) * P * STEPS],
+                    in_=rows[:].rearrange("r w l -> r (w l)"),
+                )
 
-        hop_to_output(nc, psum, stage, x_codes, x_scales, adj_codes, adj_scales, x1_rows)
         hop_to_output(nc, psum, stage, x1_codes, x1_scales, adj_codes, adj_scales, x2_rows)

@@ -70,7 +70,7 @@ def tile_avwgcn_pb_kernel(tc, x, adj, out_0, out_1):
         name="mid", bufs=6
     ) as mid, tc.tile_pool(name="stage", bufs=4) as stage, tc.psum_pool(
         name="psum", bufs=8
-    ) as psum:
+    ) as psum, tc.manual_schedule():
         identity = keep.tile([P, P], F32, name="identity")
         make_identity(nc, identity[:])
 
@@ -139,14 +139,10 @@ def tile_avwgcn_pb_kernel(tc, x, adj, out_0, out_1):
                             start=(c == 0),
                             stop=(c == PASSES - 1),
                         )
-                    copy_out(nc, (g * PACK + t) % 3 != 2, x1_t[:, t], bank[:])
-                nc.gpsimd.tensor_scalar(
+                    nc.scalar.copy(out=x1_t[:, t], in_=bank[:])
+                nc.vector.tensor_copy(
                     out=x1_grouped[:, c2, steps],
-                    in0=x1_t[:].rearrange("p t i r -> p i r t"),
-                    scalar1=1.0,
-                    scalar2=0.0,
-                    op0=mybir.AluOpType.mult,
-                    op1=mybir.AluOpType.add,
+                    in_=x1_t[:].rearrange("p t i r -> p i r t"),
                 )
                 nc.vector.quantize_mx(
                     out=x1_codes[:, c2, steps].rearrange("p l r -> p (l r)").bitcast(FP8X4),

@@ -28,6 +28,21 @@ def copy_out(nc, on_scalar, out, in_):
         nc.vector.tensor_copy(out=out, in_=in_)
 
 
+def regroup(nc, grouped, planes):
+    nc.vector.tensor_copy(
+        out=grouped.rearrange("p (n j) t -> p n t j", j=4),
+        in_=planes.rearrange("p t (n j) -> p n t j", j=4),
+    )
+
+
+def quantise(nc, codes, scales, grouped):
+    nc.vector.quantize_mx(
+        out=codes.bitcast(FP8X4),
+        scales=scales,
+        in_=grouped.rearrange("p n t -> p (n t)"),
+    )
+
+
 def hop_to_output(nc, psum, stage, feat_codes, feat_scales, adj_codes, adj_scales, out_rows):
     for wt in range(NODE_TILES):
         w_cols = slice(wt * P, (wt + 1) * P)
@@ -35,12 +50,12 @@ def hop_to_output(nc, psum, stage, feat_codes, feat_scales, adj_codes, adj_scale
         for g in range(STEP_GROUPS):
             bank = psum.tile([ROWS, QUARTERS, P], F32, name="bank", tag="bank")
             for i in range(QUARTERS):
-                step = g * QUARTERS + i
+                step_cols = slice((g * QUARTERS + i) * ROWS, (g * QUARTERS + i + 1) * ROWS)
                 for c in range(PASSES):
                     nc.tensor.matmul_mx(
                         out=bank[:, i, :],
-                        lhsT=feat_codes[:, c, step, :].bitcast(FP8X4),
-                        lhsT_scale=feat_scales[:, c, step, :],
+                        lhsT=feat_codes[:, c, step_cols].bitcast(FP8X4),
+                        lhsT_scale=feat_scales[:, c, step_cols],
                         rhs=adj_codes[:, c, w_cols].bitcast(FP8X4),
                         rhs_scale=adj_scales[:, c, w_cols],
                         start=(c == 0),
@@ -60,111 +75,83 @@ def hop_to_output(nc, psum, stage, feat_codes, feat_scales, adj_codes, adj_scale
 
 def tile_avwgcn_pb_kernel(tc, x, adj, out_0, out_1):
     nc = tc.nc
-    x_rows = x.rearrange("b c v l -> (b c) (v l)")
+    x_rows = x.rearrange("b c (n p) l -> (b c) n (p l)", p=P)
     adj_rows = adj.rearrange("(c t p) w -> p c t w", c=PASSES, t=PACK, p=P)
     x1_rows = out_0.rearrange("b c w l -> (b c) (w l)")
     x2_rows = out_1.rearrange("b c w l -> (b c) (w l)")
-    half = NODES * STEPS // PASSES
+    group_cols = QUARTERS * ROWS
 
     with tc.tile_pool(name="keep", bufs=1) as keep, tc.tile_pool(
-        name="mid", bufs=6
-    ) as mid, tc.tile_pool(name="stage", bufs=4) as stage, tc.psum_pool(
+        name="mid", bufs=3
+    ) as mid, tc.tile_pool(name="stage", bufs=6) as stage, tc.psum_pool(
         name="psum", bufs=8
-    ) as psum, tc.manual_schedule():
+    ) as psum:
         identity = keep.tile([P, P], F32, name="identity")
         make_identity(nc, identity[:])
 
         adj_raw = keep.tile([P, PASSES, PACK, NODES], BF16, name="adj_raw")
-        x_raw = keep.tile([ROWS, PASSES, half], BF16, name="x_raw")
+        x_raw = keep.tile([ROWS, NODE_TILES, P * STEPS], BF16, name="x_raw")
         for c in range(PASSES):
             nc.sync.dma_start(out=adj_raw[:, c], in_=adj_rows[:, c])
-        for c in range(PASSES):
-            nc.sync.dma_start(out=x_raw[:, c, :], in_=x_rows[:, c * half : (c + 1) * half])
+        for n in range(NODE_TILES):
+            nc.sync.dma_start(out=x_raw[:, n, :], in_=x_rows[:, n, :])
 
         adj_grouped = keep.tile([P, PASSES, NODES, PACK], BF16, name="adj_grouped", align_bytes=64)
         adj_codes = keep.tile([P, PASSES, NODES], U32, name="adj_codes", align_bytes=64)
         adj_scales = keep.tile([P, PASSES, NODES], U8, name="adj_scales", align_bytes=64)
         for c in range(PASSES):
-            nc.vector.tensor_copy(
-                out=adj_grouped[:, c].rearrange("p (n i) t -> p n t i", i=4),
-                in_=adj_raw[:, c].rearrange("p t (n i) -> p n t i", i=4),
-            )
+            regroup(nc, adj_grouped[:, c], adj_raw[:, c])
         for c in range(PASSES):
-            nc.vector.quantize_mx(
-                out=adj_codes[:, c, :].bitcast(FP8X4),
-                scales=adj_scales[:, c, :],
-                in_=adj_grouped[:, c].rearrange("p w t -> p (w t)"),
-            )
+            quantise(nc, adj_codes[:, c, :], adj_scales[:, c, :], adj_grouped[:, c])
 
-        x_words = x_raw[:].bitcast(F32).rearrange("r c (t p q) -> r c t p q", t=PACK, p=P, q=PAIRS)
-        x_grouped = keep.tile([P, PASSES, STEPS, ROWS, PACK], BF16, name="x_grouped", align_bytes=64)
-        x_codes = keep.tile([P, PASSES, STEPS, ROWS], U32, name="x_codes", align_bytes=64)
-        x_scales = keep.tile([P, PASSES, STEPS, ROWS], U8, name="x_scales", align_bytes=64)
+        x_words = x_raw[:].bitcast(F32).rearrange("r n (p q) -> r n p q", q=PAIRS)
+        x_grouped = keep.tile([P, PASSES, STEPS * ROWS, PACK], BF16, name="x_grouped", align_bytes=64)
+        x_codes = keep.tile([P, PASSES, STEPS * ROWS], U32, name="x_codes", align_bytes=64)
+        x_scales = keep.tile([P, PASSES, STEPS * ROWS], U8, name="x_scales", align_bytes=64)
         for c in range(PASSES):
+            banks = []
             for q in range(PAIRS):
                 bank = psum.tile([P, PACK, ROWS], F32, name="bank", tag="bank")
-                for t in range(PACK):
-                    nc.tensor.transpose(bank[:, t, :], x_words[:, c, t, :, q], identity[:])
+                banks.append(bank)
+            for t in range(PACK):
+                for q in range(PAIRS):
+                    nc.tensor.transpose(banks[q][:, t, :], x_words[:, c * PACK + t, :, q], identity[:])
+            for q in range(PAIRS):
                 copy_out(
                     nc,
-                    q % 3 != 2,
-                    x_grouped[:, c, 2 * q : 2 * q + 2],
-                    bank[:].bitcast(BF16).rearrange("p t (r e) -> p e r t", e=2),
+                    q % 2 == 0,
+                    x_grouped[:, c, 2 * q * ROWS : (2 * q + 2) * ROWS, :].rearrange(
+                        "p (e r) t -> p e r t", e=2
+                    ),
+                    banks[q][:].bitcast(BF16).rearrange("p t (r e) -> p e r t", e=2),
                 )
-                nc.vector.quantize_mx(
-                    out=x_codes[:, c, 2 * q : 2 * q + 2].rearrange("p l r -> p (l r)").bitcast(FP8X4),
-                    scales=x_scales[:, c, 2 * q : 2 * q + 2].rearrange("p l r -> p (l r)"),
-                    in_=x_grouped[:, c, 2 * q : 2 * q + 2].rearrange("p l r t -> p (l r t)"),
-                )
-
-        x1_grouped = keep.tile([P, PASSES, STEPS, ROWS, PACK], BF16, name="x1_grouped", align_bytes=64)
-        x1_codes = keep.tile([P, PASSES, STEPS, ROWS], U32, name="x1_codes", align_bytes=64)
-        x1_scales = keep.tile([P, PASSES, STEPS, ROWS], U8, name="x1_scales", align_bytes=64)
-        for c2 in range(PASSES):
-            sums = []
             for g in range(STEP_GROUPS):
-                steps = slice(g * QUARTERS, (g + 1) * QUARTERS)
-                x1_t = mid.tile([P, PACK, QUARTERS, ROWS], F32, name="x1_t")
-                sums.append(x1_t)
+                cols = slice(g * group_cols, (g + 1) * group_cols)
+                quantise(nc, x_codes[:, c, cols], x_scales[:, c, cols], x_grouped[:, c, cols, :])
+
+        x1_grouped = keep.tile([P, PASSES, STEPS * ROWS, PACK], BF16, name="x1_grouped", align_bytes=64)
+        x1_codes = keep.tile([P, PASSES, STEPS * ROWS], U32, name="x1_codes", align_bytes=64)
+        x1_scales = keep.tile([P, PASSES, STEPS * ROWS], U8, name="x1_scales", align_bytes=64)
+        for c2 in range(PASSES):
+            for g in range(STEP_GROUPS):
+                cols = slice(g * group_cols, (g + 1) * group_cols)
+                x1_planes = mid.tile([P, PACK, group_cols], BF16, name="x1_planes")
                 for t in range(PACK):
                     w_cols = slice((c2 * PACK + t) * P, (c2 * PACK + t + 1) * P)
-                    bank = psum.tile([P, QUARTERS, ROWS], F32, name="bank", tag="bank")
+                    bank = psum.tile([P, group_cols], F32, name="bank", tag="bank")
                     for c in range(PASSES):
                         nc.tensor.matmul_mx(
-                            out=bank[:].rearrange("p i r -> p (i r)"),
+                            out=bank[:],
                             lhsT=adj_codes[:, c, w_cols].bitcast(FP8X4),
                             lhsT_scale=adj_scales[:, c, w_cols],
-                            rhs=x_codes[:, c, steps].rearrange("p l r -> p (l r)").bitcast(FP8X4),
-                            rhs_scale=x_scales[:, c, steps].rearrange("p l r -> p (l r)"),
+                            rhs=x_codes[:, c, cols].bitcast(FP8X4),
+                            rhs_scale=x_scales[:, c, cols],
                             start=(c == 0),
                             stop=(c == PASSES - 1),
                         )
-                    nc.scalar.copy(out=x1_t[:, t], in_=bank[:])
-                nc.vector.tensor_copy(
-                    out=x1_grouped[:, c2, steps],
-                    in_=x1_t[:].rearrange("p t i r -> p i r t"),
-                )
-                nc.vector.quantize_mx(
-                    out=x1_codes[:, c2, steps].rearrange("p l r -> p (l r)").bitcast(FP8X4),
-                    scales=x1_scales[:, c2, steps].rearrange("p l r -> p (l r)"),
-                    in_=x1_grouped[:, c2, steps].rearrange("p l r t -> p (l r t)"),
-                )
-            for t in range(PACK):
-                wt = c2 * PACK + t
-                rows = stage.tile([ROWS, P, STEPS], F32, name="rows")
-                for g in range(STEP_GROUPS):
-                    bank = psum.tile([ROWS, QUARTERS, P], F32, name="bank", tag="bank")
-                    for i in range(QUARTERS):
-                        nc.tensor.transpose(bank[:, i, :], sums[g][:, t, i, :], identity[:])
-                    copy_out(
-                        nc,
-                        wt % 2 == 0,
-                        rows[:, :, g * QUARTERS : (g + 1) * QUARTERS],
-                        bank[:].rearrange("r i w -> r w i"),
-                    )
-                nc.sync.dma_start(
-                    out=x1_rows[:, wt * P * STEPS : (wt + 1) * P * STEPS],
-                    in_=rows[:].rearrange("r w l -> r (w l)"),
-                )
+                    copy_out(nc, t != PACK - 1, x1_planes[:, t, :], bank[:])
+                regroup(nc, x1_grouped[:, c2, cols, :], x1_planes[:])
+                quantise(nc, x1_codes[:, c2, cols], x1_scales[:, c2, cols], x1_grouped[:, c2, cols, :])
 
+        hop_to_output(nc, psum, stage, x_codes, x_scales, adj_codes, adj_scales, x1_rows)
         hop_to_output(nc, psum, stage, x1_codes, x1_scales, adj_codes, adj_scales, x2_rows)

import concourse.mybir as mybir
from concourse.masks import make_identity

F32 = mybir.dt.float32
BF16 = mybir.dt.bfloat16
U32 = mybir.dt.uint32
U8 = mybir.dt.uint8
FP8X4 = mybir.dt.float8_e4m3fn_x4

P = 128
PACK = 4
NODES = 1024
STEPS = 12
ROWS = 128
PASSES = NODES // (P * PACK)
NODE_TILES = NODES // P
PAIRS = STEPS // 2
QUARTERS = 4
STEP_GROUPS = STEPS // QUARTERS

FLOPS = 2 * 2 * ROWS * STEPS * NODES * NODES


def copy_out(nc, on_scalar, out, in_):
    if on_scalar:
        nc.scalar.copy(out=out, in_=in_)
    else:
        nc.vector.tensor_copy(out=out, in_=in_)


def regroup(nc, grouped, planes):
    nc.vector.tensor_copy(
        out=grouped.rearrange("p (n j) t -> p n t j", j=4),
        in_=planes.rearrange("p t (n j) -> p n t j", j=4),
    )


def quantise(nc, codes, scales, grouped):
    nc.vector.quantize_mx(
        out=codes.bitcast(FP8X4),
        scales=scales,
        in_=grouped.rearrange("p n t -> p (n t)"),
    )


def hop_to_output(nc, psum, stage, feat_codes, feat_scales, adj_codes, adj_scales, out_rows):
    for wt in range(NODE_TILES):
        w_cols = slice(wt * P, (wt + 1) * P)
        rows = stage.tile([ROWS, P, STEPS], F32, name="rows")
        for g in range(STEP_GROUPS):
            bank = psum.tile([ROWS, QUARTERS, P], F32, name="bank", tag="bank")
            for i in range(QUARTERS):
                step_cols = slice((g * QUARTERS + i) * ROWS, (g * QUARTERS + i + 1) * ROWS)
                for c in range(PASSES):
                    nc.tensor.matmul_mx(
                        out=bank[:, i, :],
                        lhsT=feat_codes[:, c, step_cols].bitcast(FP8X4),
                        lhsT_scale=feat_scales[:, c, step_cols],
                        rhs=adj_codes[:, c, w_cols].bitcast(FP8X4),
                        rhs_scale=adj_scales[:, c, w_cols],
                        start=(c == 0),
                        stop=(c == PASSES - 1),
                    )
            copy_out(
                nc,
                wt % 2 == 0,
                rows[:, :, g * QUARTERS : (g + 1) * QUARTERS],
                bank[:].rearrange("r i w -> r w i"),
            )
        nc.sync.dma_start(
            out=out_rows[:, wt * P * STEPS : (wt + 1) * P * STEPS],
            in_=rows[:].rearrange("r w l -> r (w l)"),
        )


def tile_avwgcn_pb_kernel(tc, x, adj, out_0, out_1):
    nc = tc.nc
    x_rows = x.rearrange("b c (n p) l -> (b c) n (p l)", p=P)
    adj_rows = adj.rearrange("(c t p) w -> p c t w", c=PASSES, t=PACK, p=P)
    x1_rows = out_0.rearrange("b c w l -> (b c) (w l)")
    x2_rows = out_1.rearrange("b c w l -> (b c) (w l)")
    group_cols = QUARTERS * ROWS

    with tc.tile_pool(name="keep", bufs=1) as keep, tc.tile_pool(
        name="mid", bufs=3
    ) as mid, tc.tile_pool(name="stage", bufs=6) as stage, tc.psum_pool(
        name="psum", bufs=8
    ) as psum:
        identity = keep.tile([P, P], F32, name="identity")
        make_identity(nc, identity[:])

        adj_raw = keep.tile([P, PASSES, PACK, NODES], BF16, name="adj_raw")
        x_raw = keep.tile([ROWS, NODE_TILES, P * STEPS], BF16, name="x_raw")
        for c in range(PASSES):
            nc.sync.dma_start(out=adj_raw[:, c], in_=adj_rows[:, c])
        for n in range(NODE_TILES):
            nc.sync.dma_start(out=x_raw[:, n, :], in_=x_rows[:, n, :])

        adj_grouped = keep.tile([P, PASSES, NODES, PACK], BF16, name="adj_grouped", align_bytes=64)
        adj_codes = keep.tile([P, PASSES, NODES], U32, name="adj_codes", align_bytes=64)
        adj_scales = keep.tile([P, PASSES, NODES], U8, name="adj_scales", align_bytes=64)
        for c in range(PASSES):
            regroup(nc, adj_grouped[:, c], adj_raw[:, c])
        for c in range(PASSES):
            quantise(nc, adj_codes[:, c, :], adj_scales[:, c, :], adj_grouped[:, c])

        x_words = x_raw[:].bitcast(F32).rearrange("r n (p q) -> r n p q", q=PAIRS)
        x_grouped = keep.tile([P, PASSES, STEPS * ROWS, PACK], BF16, name="x_grouped", align_bytes=64)
        x_codes = keep.tile([P, PASSES, STEPS * ROWS], U32, name="x_codes", align_bytes=64)
        x_scales = keep.tile([P, PASSES, STEPS * ROWS], U8, name="x_scales", align_bytes=64)
        for c in range(PASSES):
            banks = []
            for q in range(PAIRS):
                bank = psum.tile([P, PACK, ROWS], F32, name="bank", tag="bank")
                banks.append(bank)
            for t in range(PACK):
                for q in range(PAIRS):
                    nc.tensor.transpose(banks[q][:, t, :], x_words[:, c * PACK + t, :, q], identity[:])
            for q in range(PAIRS):
                copy_out(
                    nc,
                    q % 2 == 0,
                    x_grouped[:, c, 2 * q * ROWS : (2 * q + 2) * ROWS, :].rearrange(
                        "p (e r) t -> p e r t", e=2
                    ),
                    banks[q][:].bitcast(BF16).rearrange("p t (r e) -> p e r t", e=2),
                )
            for g in range(STEP_GROUPS):
                cols = slice(g * group_cols, (g + 1) * group_cols)
                quantise(nc, x_codes[:, c, cols], x_scales[:, c, cols], x_grouped[:, c, cols, :])

        x1_grouped = keep.tile([P, PASSES, STEPS * ROWS, PACK], BF16, name="x1_grouped", align_bytes=64)
        x1_codes = keep.tile([P, PASSES, STEPS * ROWS], U32, name="x1_codes", align_bytes=64)
        x1_scales = keep.tile([P, PASSES, STEPS * ROWS], U8, name="x1_scales", align_bytes=64)
        for c2 in range(PASSES):
            for g in range(STEP_GROUPS):
                cols = slice(g * group_cols, (g + 1) * group_cols)
                x1_planes = mid.tile([P, PACK, group_cols], BF16, name="x1_planes")
                for t in range(PACK):
                    w_cols = slice((c2 * PACK + t) * P, (c2 * PACK + t + 1) * P)
                    bank = psum.tile([P, group_cols], F32, name="bank", tag="bank")
                    for c in range(PASSES):
                        nc.tensor.matmul_mx(
                            out=bank[:],
                            lhsT=adj_codes[:, c, w_cols].bitcast(FP8X4),
                            lhsT_scale=adj_scales[:, c, w_cols],
                            rhs=x_codes[:, c, cols].bitcast(FP8X4),
                            rhs_scale=x_scales[:, c, cols],
                            start=(c == 0),
                            stop=(c == PASSES - 1),
                        )
                    copy_out(nc, t != PACK - 1, x1_planes[:, t, :], bank[:])
                regroup(nc, x1_grouped[:, c2, cols, :], x1_planes[:])
                quantise(nc, x1_codes[:, c2, cols], x1_scales[:, c2, cols], x1_grouped[:, c2, cols, :])

        hop_to_output(nc, psum, stage, x_codes, x_scales, adj_codes, adj_scales, x1_rows)
        hop_to_output(nc, psum, stage, x1_codes, x1_scales, adj_codes, adj_scales, x2_rows)
